import numpy as np
import ml_dtypes


def mxq(x, axis, fmt="e4m3"):
    dtype, down = {"e4m3": (ml_dtypes.float8_e4m3fn, 7), "e5m2": (ml_dtypes.float8_e5m2, 14)}[fmt]
    v = np.moveaxis(np.asarray(x, np.float32).astype(ml_dtypes.bfloat16).astype(np.float64), axis, -1)
    blocks = v.reshape(v.shape[:-1] + (-1, 32))
    amax = np.abs(blocks).max(-1, keepdims=True)
    byte = np.maximum(np.where(amax > 0, np.frexp(amax)[1] - 1 + 127, 0) - down, 1)
    scale = np.exp2(byte - 127.0)
    codes = (blocks / scale).astype(np.float32).astype(dtype).astype(np.float64)
    return np.moveaxis((codes * scale).reshape(v.shape), -1, axis)


WIDE = False


def mx_kscale(k):
    if not WIDE:
        return np.ones(k)
    levels = np.array([10, -10, 5, -5, 0])
    if k % 512:
        return np.exp2(np.random.permutation(np.resize(levels, k // 32))).repeat(32)
    a = np.empty((k // 512, 16))
    for p in range(k // 512):
        a[p, :8] = np.random.permutation(np.resize(levels, 8))
        for g in range(8):
            far = levels[np.abs(levels - a[p, g]) >= 10]
            a[p, g + 8] = far[np.random.randint(len(far))]
    return np.exp2(a.ravel()).repeat(32)


BF16 = ml_dtypes.bfloat16


def bf(x):
    return np.asarray(x, np.float32).astype(BF16)


def f64(x):
    return np.asarray(x).astype(np.float64)


B, S, H, I = 2, 256, 1024, 3072


def silu(v):
    return v / (1.0 + np.exp(-v))


def ternary(shape):
    return np.random.randint(-1, 2, shape).astype(np.float64)


def setup_inputs():
    s, t = mx_kscale(H), mx_kscale(I)
    x = np.random.standard_normal((B, S, H)) * s
    gate_w = ternary((I, H)) / s[None, :]
    up_w = ternary((I, H)) / s[None, :]
    down_w = ternary((H, I)) / t[None, :]
    gate_s = np.random.uniform(0.5, 2.5, I) / np.sqrt(H)
    up_s = np.random.uniform(0.5, 2.5, I) / np.sqrt(H) * t
    down_s = np.random.uniform(0.5, 2.5, H) / np.sqrt(I)
    return {"x": bf(x), "gate_w": bf(gate_w), "up_w": bf(up_w), "down_w": bf(down_w),
            "gate_s": bf(gate_s), "up_s": bf(up_s), "down_s": bf(down_s)}


def reference(x, gate_w, up_w, down_w, gate_s, up_s, down_s):
    x = f64(x)
    b, s, h = x.shape
    xq = mxq(x.reshape(b * s, h), 1, "e4m3")
    g = (xq @ mxq(f64(gate_w), 1, "e4m3").T) * f64(gate_s)
    u = (xq @ mxq(f64(up_w), 1, "e4m3").T) * f64(up_s)
    hdn = silu(g) * u
    out = (mxq(hdn, 1, "e4m3") @ mxq(f64(down_w), 1, "e4m3").T) * f64(down_s)
    return out.reshape(b, s, -1)

@@ -1,0 +1,361 @@
+from contextlib import ExitStack
+
+import concourse.mybir as mybir
+from concourse.masks import make_identity
+
+F32 = mybir.dt.float32
+BF16 = mybir.dt.bfloat16
+U32 = mybir.dt.uint32
+U8 = mybir.dt.uint8
+FP8X4 = mybir.dt.float8_e4m3fn_x4
+SILU = mybir.ActivationFunctionType.Silu
+MULT = mybir.AluOpType.mult
+
+P = 128
+TOK = 512
+H = 1024
+INNER = 3072
+UNITS = INNER // 256
+G2 = INNER // 512
+W_BUFS = 6
+FLOPS = 2 * TOK * H * 2 * INNER + 2 * TOK * INNER * H
+
+
+def tile_cudaternaryexpertmodule_kernel(
+    tc, x, gate_w, up_w, down_w, gate_s, up_s, down_s, out
+):
+    nc = tc.nc
+    xf = x.flatten_outer_dims()
+    of = out.flatten_outer_dims()
+    gate_rows = gate_w.rearrange("(g p b e) h -> g b p (e h)", p=P, b=2, e=2)
+    up_rows = up_w.rearrange("(g p b e) h -> g b p (e h)", p=P, b=2, e=2)
+    down_rows = down_w.rearrange("(b p) k -> b p k", p=P)
+
+    with ExitStack() as ctx:
+        const = ctx.enter_context(tc.tile_pool(name="const", bufs=1))
+        wpool = ctx.enter_context(tc.tile_pool(name="wpool", bufs=W_BUFS))
+        dpool = ctx.enter_context(tc.tile_pool(name="dpool", bufs=8))
+        spool = ctx.enter_context(tc.tile_pool(name="stage", bufs=3))
+        cpool = ctx.enter_context(tc.tile_pool(name="codes", bufs=3))
+        dcpool = ctx.enter_context(tc.tile_pool(name="dcodes", bufs=2))
+        epool = ctx.enter_context(tc.tile_pool(name="epi", bufs=2))
+        opool = ctx.enter_context(tc.tile_pool(name="outs", bufs=4))
+        psum = ctx.enter_context(tc.psum_pool(name="psum", bufs=1))
+        ctx.enter_context(tc.manual_schedule())
+
+        def fill(bank_no, label, srcs):
+            bk = psum.tile([P, 512], F32, name=label, tag="bank%d" % bank_no)
+            for n, src in enumerate(srcs):
+                nc.tensor.transpose(bk[:, P * n : P * (n + 1)], src, ident[:])
+            return bk
+
+        def evac(eng, dst4, bk):
+            src4 = bk[:].rearrange("p (a u m) -> p a m u", a=2, u=2, m=P)
+            if eng == "s":
+                nc.scalar.copy(out=dst4, in_=src4)
+            else:
+                nc.vector.tensor_copy(out=dst4, in_=src4)
+
+        def words512(stg, n):
+            return (
+                stg[:]
+                .bitcast(F32)[:, 512 * n : 512 * (n + 1)]
+                .rearrange("p (a m u) -> p a m u", a=2, m=P, u=2)
+            )
+
+        def quantise(stg, half, codes, scales, first_word):
+            nc.vector.quantize_mx(
+                out=codes[:, first_word : first_word + 512].bitcast(FP8X4),
+                scales=scales[:, first_word : first_word + 512],
+                in_=stg[:, 2048 * half : 2048 * (half + 1)],
+            )
+
+        warm = const.tile([P, 1], F32, name="warm")
+        warm_out = const.tile([P, 1], F32, name="warm_out")
+        nc.vector.memset(warm[:], 0.0)
+        sc_raw = const.tile([P, 512], BF16, name="sc_raw")
+        nc.vector.memset(sc_raw[:], 0.0)
+        ident = const.tile([P, P], F32, name="ident")
+        make_identity(nc, ident[:])
+        nc.scalar.dma_start(out=sc_raw[0:6, :], in_=gate_s.rearrange("(a w) -> a w", a=G2))
+        nc.scalar.dma_start(out=sc_raw[6:12, :], in_=up_s.rearrange("(a w) -> a w", a=G2))
+        nc.scalar.activation(out=warm_out[:], in_=warm[:], func=SILU)
+
+        x_sb = []
+        for tt in range(4):
+            xt = const.tile([P, H], BF16, name="x%d" % tt)
+            nc.sync.dma_start(out=xt[:], in_=xf[P * tt : P * (tt + 1), :])
+            x_sb.append(xt)
+
+        gw = {}
+        uw = {}
+
+        def load_gu(a):
+            g = wpool.tile([P, 2 * H], BF16, name="gw%d" % a, tag="gw")
+            nc.sync.dma_start(out=g[:], in_=gate_rows[a // 2, a % 2])
+            u = wpool.tile([P, 2 * H], BF16, name="uw%d" % a, tag="uw")
+            nc.sync.dma_start(out=u[:], in_=up_rows[a // 2, a % 2])
+            gw[a] = g
+            uw[a] = u
+
+        for a in range(W_BUFS):
+            load_gu(a)
+
+        dw = []
+        ds_bc = const.tile([P, H], BF16, name="ds_bc")
+
+        def load_down():
+            for b in range(8):
+                d = dpool.tile([P, INNER], BF16, name="dw%d" % b, tag="dw")
+                nc.sync.dma_start(out=d[:], in_=down_rows[b])
+                dw.append(d)
+            nc.sync.dma_start(out=ds_bc[:], in_=down_s.partition_broadcast(P))
+
+        xc = const.tile([P, 1024], U32, name="xc", align_bytes=64)
+        xs = const.tile([P, 1024], U8, name="xs", align_bytes=64)
+        hc = const.tile([P, G2 * 512], U32, name="hc", align_bytes=64)
+        hs = const.tile([P, G2 * 512], U8, name="hs", align_bytes=64)
+        sc_w = const.tile([P, 24], F32, name="sc_w")
+        sc_f = const.tile([P, 48], F32, name="sc_f")
+
+        stg_of = {}
+        wc_of = {}
+
+        def transpose_unit(a, banks):
+            bks = []
+            for j, (w, e) in enumerate(((gw[a], 0), (uw[a], 0), (gw[a], 1), (uw[a], 1))):
+                words = w[:].bitcast(F32)
+                srcs = [
+                    words[:, 512 * e + 256 * g + v : 512 * e + 256 * (g + 1) : 2]
+                    for g in range(2)
+                    for v in range(2)
+                ]
+                bks.append(fill(banks[j], "t%d_%d" % (a, j), srcs))
+            if a + W_BUFS < UNITS:
+                load_gu(a + W_BUFS)
+                if a + W_BUFS == UNITS - 1:
+                    load_down()
+            stg = spool.tile([P, 4096], BF16, name="stg%d" % a, tag="stg", align_bytes=64)
+            stg_of[a] = stg
+            return bks
+
+        def new_codes(a):
+            wc = cpool.tile([P, 1024], U32, name="wc%d" % a, tag="wc", align_bytes=64)
+            ws = cpool.tile([P, 1024], U8, name="ws%d" % a, tag="ws", align_bytes=64)
+            wc_of[a] = (wc, ws)
+
+        def quantise_unit(a, half):
+            wc, ws = wc_of[a]
+            quantise(stg_of[a], half, wc, ws, 512 * half)
+
+        def mx_unit(a):
+            wc, ws = wc_of[a]
+            bks = []
+            for j in range(4):
+                bk = psum.tile([P, 512], F32, name="m%d_%d" % (a, j), tag="bank%d" % (4 + j))
+                for g in range(2):
+                    c0 = 256 * j + P * g
+                    nc.tensor.matmul_mx(
+                        out=bk[:],
+                        lhsT=wc[:, c0 : c0 + P].bitcast(FP8X4),
+                        lhsT_scale=ws[:, c0 : c0 + P],
+                        rhs=xc[:, 512 * g : 512 * (g + 1)].bitcast(FP8X4),
+                        rhs_scale=xs[:, 512 * g : 512 * (g + 1)],
+                        start=(g == 0),
+                        stop=(g == 1),
+                    )
+                bks.append(bk)
+            return bks
+
+        sl_of = {}
+        hsb_of = {}
+        hg_of = {}
+
+        def silu(a, e, bks):
+            sl = epool.tile([P, 512], F32, name="sl%d_%d" % (a, e), tag="sl", bufs=3)
+            c = 24 * (a % 2) + 2 * (a // 2) + e
+            nc.scalar.activation(out=sl[:], in_=bks[2 * e][:], func=SILU, scale=sc_f[:, c : c + 1])
+            sl_of[e] = sl
+
+        def product(a, e, bks):
+            if a % 2 == 0 and e == 0:
+                hsb = epool.tile([P, 2048], BF16, name="hsb%d" % (a // 2), tag="hsb")
+                hsb_of[a // 2] = hsb
+            t = 2 * (a % 2) + e
+            c = 24 * (a % 2) + 12 + 2 * (a // 2) + e
+            nc.vector.scalar_tensor_tensor(
+                out=hsb_of[a // 2][:, 512 * t : 512 * (t + 1)],
+                in0=bks[2 * e + 1][:],
+                scalar=sc_f[:, c : c + 1],
+                in1=sl_of[e][:],
+                op0=MULT,
+                op1=MULT,
+            )
+
+        def regroup(g2):
+            hg = epool.tile([P, 2048], BF16, name="hg%d" % g2, tag="hg", align_bytes=64)
+            hg_of[g2] = hg
+            nc.vector.tensor_copy(
+                out=hg[:].rearrange("p (c i t) -> p c t i", c=P, i=4, t=4),
+                in_=hsb_of[g2][:].rearrange("p (t c i) -> p c t i", t=4, c=P, i=4),
+            )
+
+        def quantise_hidden(g2):
+            nc.vector.quantize_mx(
+                out=hc[:, 512 * g2 : 512 * (g2 + 1)].bitcast(FP8X4),
+                scales=hs[:, 512 * g2 : 512 * (g2 + 1)],
+                in_=hg_of[g2][:],
+            )
+
+        dstg_of = {}
+        dc_of = {}
+
+        def down_fill(q, g2, bank_no):
+            srcs = []
+            for bb in range(2):
+                words = dw[2 * q + bb][:].bitcast(F32)
+                for u in range(2):
+                    srcs.append(words[:, 256 * g2 + u : 256 * (g2 + 1) : 2])
+            return fill(bank_no, "d%d_%d" % (q, g2), srcs)
+
+        def down_evac(eng, q, g2, bk):
+            if g2 % 4 == 0:
+                stg = spool.tile(
+                    [P, 4096], BF16, name="dstg%d_%d" % (q, g2 // 4), tag="stg", align_bytes=64
+                )
+                dstg_of[(q, g2 // 4)] = stg
+            evac(eng, words512(dstg_of[(q, g2 // 4)], g2 % 4), bk)
+
+        def down_quantise(q, pair):
+            if pair == 0:
+                dc = dcpool.tile([P, G2 * 256], U32, name="dc%d" % q, tag="dc", align_bytes=64)
+                dsc = dcpool.tile([P, G2 * 256], U8, name="dsc%d" % q, tag="dsc", align_bytes=64)
+                dc_of[q] = (dc, dsc)
+            dc, dsc = dc_of[q]
+            quantise(dstg_of[(q, pair // 2)], pair % 2, dc, dsc, 512 * pair)
+
+        def mx2_pass(q, tt, g2, dst):
+            dc, dsc = dc_of[q]
+            c0 = 512 * g2 + P * tt
+            nc.tensor.matmul_mx(
+                out=dst,
+                lhsT=hc[:, c0 : c0 + P].bitcast(FP8X4),
+                lhsT_scale=hs[:, c0 : c0 + P],
+                rhs=dc[:, 256 * g2 : 256 * (g2 + 1)].bitcast(FP8X4),
+                rhs_scale=dsc[:, 256 * g2 : 256 * (g2 + 1)],
+                start=(g2 == 0),
+                stop=(g2 == G2 - 1),
+            )
+
+        def final(q, tt, src):
+            o = opool.tile([P, 256], F32, name="o%d_%d" % (q, tt), tag="o")
+            nc.vector.tensor_tensor(
+                out=o[:], in0=src, in1=ds_bc[:, 256 * q : 256 * (q + 1)], op=MULT
+            )
+            nc.sync.dma_start(
+                out=of[P * tt : P * (tt + 1), 256 * q : 256 * (q + 1)], in_=o[:]
+            )
+
+        xg = spool.tile([P, 4096], BF16, name="xg", tag="stg", align_bytes=64)
+        xg4 = xg[:].bitcast(F32).rearrange("p (g w u) -> p g w u", g=2, w=TOK, u=2)
+        for tt in range(4):
+            words = x_sb[tt][:].bitcast(F32)
+            srcs = [words[:, 256 * g + v : 256 * (g + 1) : 2] for g in range(2) for v in range(2)]
+            bk = fill(tt, "tx%d" % tt, srcs)
+            evac("v" if tt % 2 == 0 else "s", xg4[:, :, P * tt : P * (tt + 1), :], bk)
+
+        bk = fill(7, "tsc", [sc_raw[:].bitcast(F32)[:, v:256:2] for v in range(2)])
+        nc.vector.tensor_copy(
+            out=sc_w[:].rearrange("p (v r) -> p v r", v=2),
+            in_=bk[:, 0:256].rearrange("p (v r) -> p v r", v=2)[:, :, 0:12],
+        )
+        nc.vector.tensor_copy(out=sc_f[:], in_=sc_w[:].bitcast(BF16))
+        quantise(xg, 0, xc, xs, 0)
+        quantise(xg, 1, xc, xs, 512)
+
+        bks = transpose_unit(0, (4, 5, 6, 7))
+        new_codes(0)
+        evac("s", words512(stg_of[0], 0), bks[0])
+        evac("s", words512(stg_of[0], 1), bks[1])
+        quantise_unit(0, 0)
+        evac("s", words512(stg_of[0], 2), bks[2])
+        evac("v", words512(stg_of[0], 3), bks[3])
+        quantise_unit(0, 1)
+
+        bks = transpose_unit(1, (0, 1, 2, 3))
+        for j in range(4):
+            evac("s", words512(stg_of[1], j), bks[j])
+
+        early = ((0, 0), (0, 1), (0, 2), (0, 3), (0, 4), (0, 5), (1, 0), (1, 1))
+        for a in range(UNITS):
+            mbks = mx_unit(a)
+            if a + 2 < UNITS:
+                tbks = transpose_unit(a + 2, (0, 1, 2, 3))
+            else:
+                part = early[4 * (a - 10) : 4 * (a - 10) + 4]
+                tbks = [down_fill(q, g2, n) for n, (q, g2) in enumerate(part)]
+            silu(a, 0, mbks)
+            silu(a, 1, mbks)
+            for j in range(4):
+                if a + 2 < UNITS:
+                    evac("s", words512(stg_of[a + 2], j), tbks[j])
+                else:
+                    q, g2 = early[4 * (a - 10) + j]
+                    down_evac("s", q, g2, tbks[j])
+            if a + 1 < UNITS:
+                new_codes(a + 1)
+                quantise_unit(a + 1, 0)
+                quantise_unit(a + 1, 1)
+            else:
+                down_quantise(0, 0)
+                down_quantise(0, 1)
+            if a % 2 == 0 and a >= 2:
+                quantise_hidden(a // 2 - 1)
+            product(a, 0, mbks)
+            product(a, 1, mbks)
+            if a % 2 == 1:
+                regroup(a // 2)
+
+        tbks = [down_fill(1, g2, 2 + g2) for g2 in range(2, 6)]
+        for g2 in range(2, 6):
+            down_evac("s", 1, g2, tbks[g2 - 2])
+        down_quantise(0, 2)
+        quantise_hidden(G2 - 1)
+        down_quantise(1, 0)
+
+        obks = []
+        for tt in range(4):
+            ob = psum.tile([P, 512], F32, name="o0_%d" % tt, tag="bank%d" % tt)
+            obks.append(ob)
+        for g2 in range(G2):
+            for tt in range(4):
+                mx2_pass(0, tt, g2, obks[tt][:, 0:256])
+        down_quantise(1, 1)
+        down_quantise(1, 2)
+        for tt in range(4):
+            final(0, tt, obks[tt][:, 0:256])
+
+        ring = (4, 5, 6, 7, 0, 1)
+        for q in (2, 3):
+            tbks = [down_fill(q, g2, ring[g2]) for g2 in range(G2)]
+            for g2 in range(G2):
+                down_evac("s" if g2 % 2 == 0 else "v", q, g2, tbks[g2])
+                if g2 == 3:
+                    down_quantise(q, 0)
+            down_quantise(q, 1)
+            down_quantise(q, 2)
+            obks = []
+            for n in range(2):
+                ob = psum.tile([P, 512], F32, name="o%d_%d" % (q - 1, n), tag="bank%d" % (2 + n))
+                obks.append(ob)
+                for half in range(2):
+                    for g2 in range(G2):
+                        mx2_pass(q - 1, 2 * n + half, g2, ob[:, 256 * half : 256 * (half + 1)])
+            for tt in range(4):
+                final(q - 1, tt, obks[tt // 2][:, 256 * (tt % 2) : 256 * (tt % 2 + 1)])
+
+        for tt in range(4):
+            ob = psum.tile([P, 512], F32, name="o3_%d" % tt, tag="bank%d" % (4 + tt))
+            for g2 in range(G2):
+                mx2_pass(3, tt, g2, ob[:, 0:256])
+            final(3, tt, ob[:, 0:256])

@@ -34,6 +34,7 @@ def tile_cudaternaryexpertmodule_kernel(
     with ExitStack() as ctx:
         const = ctx.enter_context(tc.tile_pool(name="const", bufs=1))
         wpool = ctx.enter_context(tc.tile_pool(name="wpool", bufs=W_BUFS))
+        ppool = ctx.enter_context(tc.tile_pool(name="ppool", bufs=3))
         dpool = ctx.enter_context(tc.tile_pool(name="dpool", bufs=8))
         spool = ctx.enter_context(tc.tile_pool(name="stage", bufs=3))
         cpool = ctx.enter_context(tc.tile_pool(name="codes", bufs=3))
@@ -121,15 +122,43 @@ def tile_cudaternaryexpertmodule_kernel(
         stg_of = {}
         wc_of = {}
 
+        pgw = {}
+        puw = {}
+
+        def split_words(w, dt):
+            return (
+                w[:].bitcast(dt).rearrange("p (b w v) -> p b v w", b=4, w=P, v=2)
+            )
+
+        def permuted_words(w, dt):
+            return (
+                w[:].bitcast(dt).rearrange("p (b v w) -> p b v w", b=4, v=2, w=P)
+            )
+
+        def permute_gate(a):
+            pg = ppool.tile([P, 2 * H], BF16, name="pg%d" % a, tag="pg")
+            nc.vector.tensor_copy(out=permuted_words(pg, F32), in_=split_words(gw[a], F32))
+            pgw[a] = pg
+
+        def permute_up(a):
+            pu = ppool.tile([P, 2 * H], BF16, name="pu%d" % a, tag="pu")
+            nc.gpsimd.tensor_copy(out=permuted_words(pu, U32), in_=split_words(uw[a], U32))
+            puw[a] = pu
+
         def transpose_unit(a, banks):
             bks = []
-            for j, (w, e) in enumerate(((gw[a], 0), (uw[a], 0), (gw[a], 1), (uw[a], 1))):
+            gsrc = pgw.get(a, gw[a])
+            usrc = puw.get(a, uw[a])
+            for j, (w, e) in enumerate(((gsrc, 0), (usrc, 0), (gsrc, 1), (usrc, 1))):
                 words = w[:].bitcast(F32)
-                srcs = [
-                    words[:, 512 * e + 256 * g + v : 512 * e + 256 * (g + 1) : 2]
-                    for g in range(2)
-                    for v in range(2)
-                ]
+                if a in pgw:
+                    srcs = [words[:, 512 * e + P * n : 512 * e + P * (n + 1)] for n in range(4)]
+                else:
+                    srcs = [
+                        words[:, 512 * e + 256 * g + v : 512 * e + 256 * (g + 1) : 2]
+                        for g in range(2)
+                        for v in range(2)
+                    ]
                 bks.append(fill(banks[j], "t%d_%d" % (a, j), srcs))
             if a + W_BUFS < UNITS:
                 load_gu(a + W_BUFS)
@@ -282,6 +311,8 @@ def tile_cudaternaryexpertmodule_kernel(
         evac("v", words512(stg_of[0], 3), bks[3])
         quantise_unit(0, 1)
 
+        permute_gate(2)
+        permute_up(2)
         bks = transpose_unit(1, (0, 1, 2, 3))
         for j in range(4):
             evac("s", words512(stg_of[1], j), bks[j])
@@ -313,6 +344,9 @@ def tile_cudaternaryexpertmodule_kernel(
                 quantise_hidden(a // 2 - 1)
             product(a, 0, mbks)
             product(a, 1, mbks)
+            if a + 3 < UNITS:
+                permute_gate(a + 3)
+                permute_up(a + 3)
             if a % 2 == 1:
                 regroup(a // 2)
 

@@ -17,7 +17,7 @@ H = 1024
 INNER = 3072
 UNITS = INNER // 256
 G2 = INNER // 512
-W_BUFS = 6
+W_BUFS = 5
 FLOPS = 2 * TOK * H * 2 * INNER + 2 * TOK * INNER * H
 
 
@@ -34,8 +34,8 @@ def tile_cudaternaryexpertmodule_kernel(
     with ExitStack() as ctx:
         const = ctx.enter_context(tc.tile_pool(name="const", bufs=1))
         wpool = ctx.enter_context(tc.tile_pool(name="wpool", bufs=W_BUFS))
-        ppool = ctx.enter_context(tc.tile_pool(name="ppool", bufs=3))
         dpool = ctx.enter_context(tc.tile_pool(name="dpool", bufs=8))
+        dppool = ctx.enter_context(tc.tile_pool(name="dppool", bufs=4))
         spool = ctx.enter_context(tc.tile_pool(name="stage", bufs=3))
         cpool = ctx.enter_context(tc.tile_pool(name="codes", bufs=3))
         dcpool = ctx.enter_context(tc.tile_pool(name="dcodes", bufs=2))
@@ -122,38 +122,36 @@ def tile_cudaternaryexpertmodule_kernel(
         stg_of = {}
         wc_of = {}
 
-        pgw = {}
-        puw = {}
+        perm_of = {}
 
-        def split_words(w, dt):
-            return (
-                w[:].bitcast(dt).rearrange("p (b w v) -> p b v w", b=4, w=P, v=2)
+        def split_words(words, blocks):
+            return words.rearrange("p (b w v) -> p b v w", b=blocks, w=P, v=2)
+
+        def sorted_words(words, blocks):
+            return words.rearrange("p (b v w) -> p b v w", b=blocks, v=2, w=P)
+
+        def permute_unit(a):
+            pp = spool.tile([P, 4096], BF16, name="pp%d" % a, tag="stg", align_bytes=64)
+            nc.gpsimd.tensor_copy(
+                out=sorted_words(pp[:, 2048:4096].bitcast(U32), 4),
+                in_=split_words(uw[a][:].bitcast(U32), 4),
             )
-
-        def permuted_words(w, dt):
-            return (
-                w[:].bitcast(dt).rearrange("p (b v w) -> p b v w", b=4, v=2, w=P)
+            nc.vector.tensor_copy(
+                out=sorted_words(pp[:, 0:2048].bitcast(F32), 4),
+                in_=split_words(gw[a][:].bitcast(F32), 4),
             )
-
-        def permute_gate(a):
-            pg = ppool.tile([P, 2 * H], BF16, name="pg%d" % a, tag="pg")
-            nc.vector.tensor_copy(out=permuted_words(pg, F32), in_=split_words(gw[a], F32))
-            pgw[a] = pg
-
-        def permute_up(a):
-            pu = ppool.tile([P, 2 * H], BF16, name="pu%d" % a, tag="pu")
-            nc.gpsimd.tensor_copy(out=permuted_words(pu, U32), in_=split_words(uw[a], U32))
-            puw[a] = pu
+            perm_of[a] = pp
 
         def transpose_unit(a, banks):
             bks = []
-            gsrc = pgw.get(a, gw[a])
-            usrc = puw.get(a, uw[a])
-            for j, (w, e) in enumerate(((gsrc, 0), (usrc, 0), (gsrc, 1), (usrc, 1))):
-                words = w[:].bitcast(F32)
-                if a in pgw:
-                    srcs = [words[:, 512 * e + P * n : 512 * e + P * (n + 1)] for n in range(4)]
+            for j in range(4):
+                e, m = j // 2, j % 2
+                if a in perm_of:
+                    words = perm_of[a][:].bitcast(F32)
+                    c0 = 1024 * m + 512 * e
+                    srcs = [words[:, c0 + P * n : c0 + P * (n + 1)] for n in range(4)]
                 else:
+                    words = (gw[a], uw[a])[m][:].bitcast(F32)
                     srcs = [
                         words[:, 512 * e + 256 * g + v : 512 * e + 256 * (g + 1) : 2]
                         for g in range(2)
@@ -224,10 +222,10 @@ def tile_cudaternaryexpertmodule_kernel(
         def regroup(g2):
             hg = epool.tile([P, 2048], BF16, name="hg%d" % g2, tag="hg", align_bytes=64)
             hg_of[g2] = hg
-            nc.vector.tensor_copy(
-                out=hg[:].rearrange("p (c i t) -> p c t i", c=P, i=4, t=4),
-                in_=hsb_of[g2][:].rearrange("p (t c i) -> p c t i", t=4, c=P, i=4),
-            )
+            dst = hg[:].rearrange("p (c i t) -> p c t i", c=P, i=4, t=4)
+            src = hsb_of[g2][:].rearrange("p (t c i) -> p c t i", t=4, c=P, i=4)
+            nc.vector.tensor_copy(out=dst[:, 0:64], in_=src[:, 0:64])
+            nc.scalar.copy(out=dst[:, 64:128], in_=src[:, 64:128])
 
         def quantise_hidden(g2):
             nc.vector.quantize_mx(
@@ -239,12 +237,29 @@ def tile_cudaternaryexpertmodule_kernel(
         dstg_of = {}
         dc_of = {}
 
+        pdw = {}
+
+        def permute_down(eng, dt, b, first, last):
+            pd = dppool.tile([P, INNER], BF16, name="pdw%d" % b, tag="pdw")
+            cols = slice(512 * first, 512 * last)
+            eng.tensor_copy(
+                out=sorted_words(pd[:, cols].bitcast(dt), last - first),
+                in_=split_words(dw[b][:, cols].bitcast(dt), last - first),
+            )
+            for g2 in range(first, last):
+                pdw[(b, g2)] = pd
+
         def down_fill(q, g2, bank_no):
             srcs = []
             for bb in range(2):
-                words = dw[2 * q + bb][:].bitcast(F32)
+                b = 2 * q + bb
                 for u in range(2):
-                    srcs.append(words[:, 256 * g2 + u : 256 * (g2 + 1) : 2])
+                    if (b, g2) in pdw:
+                        c0 = 256 * g2 + P * u
+                        srcs.append(pdw[(b, g2)][:].bitcast(F32)[:, c0 : c0 + P])
+                    else:
+                        words = dw[b][:].bitcast(F32)
+                        srcs.append(words[:, 256 * g2 + u : 256 * (g2 + 1) : 2])
             return fill(bank_no, "d%d_%d" % (q, g2), srcs)
 
         def down_evac(eng, q, g2, bk):
@@ -293,12 +308,6 @@ def tile_cudaternaryexpertmodule_kernel(
             bk = fill(tt, "tx%d" % tt, srcs)
             evac("v" if tt % 2 == 0 else "s", xg4[:, :, P * tt : P * (tt + 1), :], bk)
 
-        bk = fill(7, "tsc", [sc_raw[:].bitcast(F32)[:, v:256:2] for v in range(2)])
-        nc.vector.tensor_copy(
-            out=sc_w[:].rearrange("p (v r) -> p v r", v=2),
-            in_=bk[:, 0:256].rearrange("p (v r) -> p v r", v=2)[:, :, 0:12],
-        )
-        nc.vector.tensor_copy(out=sc_f[:], in_=sc_w[:].bitcast(BF16))
         quantise(xg, 0, xc, xs, 0)
         quantise(xg, 1, xc, xs, 512)
 
@@ -311,11 +320,17 @@ def tile_cudaternaryexpertmodule_kernel(
         evac("v", words512(stg_of[0], 3), bks[3])
         quantise_unit(0, 1)
 
-        permute_gate(2)
-        permute_up(2)
         bks = transpose_unit(1, (0, 1, 2, 3))
+        permute_unit(2)
         for j in range(4):
             evac("s", words512(stg_of[1], j), bks[j])
+
+        bk = fill(7, "tsc", [sc_raw[:].bitcast(F32)[:, v:256:2] for v in range(2)])
+        nc.vector.tensor_copy(
+            out=sc_w[:].rearrange("p (v r) -> p v r", v=2),
+            in_=bk[:, 0:256].rearrange("p (v r) -> p v r", v=2)[:, :, 0:12],
+        )
+        nc.vector.tensor_copy(out=sc_f[:], in_=sc_w[:].bitcast(BF16))
 
         early = ((0, 0), (0, 1), (0, 2), (0, 3), (0, 4), (0, 5), (1, 0), (1, 1))
         for a in range(UNITS):
@@ -345,8 +360,11 @@ def tile_cudaternaryexpertmodule_kernel(
             product(a, 0, mbks)
             product(a, 1, mbks)
             if a + 3 < UNITS:
-                permute_gate(a + 3)
-                permute_up(a + 3)
+                permute_unit(a + 3)
+            if a == 9:
+                permute_down(nc.gpsimd, U32, 2, 2, 6)
+            if a == 10:
+                permute_down(nc.gpsimd, U32, 3, 2, 6)
             if a % 2 == 1:
                 regroup(a // 2)
 
@@ -356,6 +374,8 @@ def tile_cudaternaryexpertmodule_kernel(
         down_quantise(0, 2)
         quantise_hidden(G2 - 1)
         down_quantise(1, 0)
+        permute_down(nc.vector, F32, 4, 0, 6)
+        permute_down(nc.vector, F32, 5, 0, 6)
 
         obks = []
         for tt in range(4):
@@ -368,12 +388,14 @@ def tile_cudaternaryexpertmodule_kernel(
         down_quantise(1, 2)
         for tt in range(4):
             final(0, tt, obks[tt][:, 0:256])
+        permute_down(nc.vector, F32, 6, 0, 6)
+        permute_down(nc.vector, F32, 7, 0, 6)
 
         ring = (4, 5, 6, 7, 0, 1)
         for q in (2, 3):
             tbks = [down_fill(q, g2, ring[g2]) for g2 in range(G2)]
             for g2 in range(G2):
-                down_evac("s" if g2 % 2 == 0 else "v", q, g2, tbks[g2])
+                down_evac("s", q, g2, tbks[g2])
                 if g2 == 3:
                     down_quantise(q, 0)
             down_quantise(q, 1)

@@ -17,7 +17,7 @@ H = 1024
 INNER = 3072
 UNITS = INNER // 256
 G2 = INNER // 512
-W_BUFS = 5
+W_BUFS = 4
 FLOPS = 2 * TOK * H * 2 * INNER + 2 * TOK * INNER * H
 
 
@@ -25,8 +25,8 @@ def tile_cudaternaryexpertmodule_kernel(
     tc, x, gate_w, up_w, down_w, gate_s, up_s, down_s, out
 ):
     nc = tc.nc
-    xf = x.flatten_outer_dims()
-    of = out.flatten_outer_dims()
+    x_rows = x.flatten_outer_dims().rearrange("(c p e) h -> c p (e h)", p=P, e=2)
+    out_rows = out.flatten_outer_dims().rearrange("(c p e) h -> c e p h", p=P, e=2)
     gate_rows = gate_w.rearrange("(g p b e) h -> g b p (e h)", p=P, b=2, e=2)
     up_rows = up_w.rearrange("(g p b e) h -> g b p (e h)", p=P, b=2, e=2)
     down_rows = down_w.rearrange("(b p) k -> b p k", p=P)
@@ -35,12 +35,12 @@ def tile_cudaternaryexpertmodule_kernel(
         const = ctx.enter_context(tc.tile_pool(name="const", bufs=1))
         wpool = ctx.enter_context(tc.tile_pool(name="wpool", bufs=W_BUFS))
         dpool = ctx.enter_context(tc.tile_pool(name="dpool", bufs=8))
-        dppool = ctx.enter_context(tc.tile_pool(name="dppool", bufs=4))
+        dppool = ctx.enter_context(tc.tile_pool(name="dppool", bufs=6))
         spool = ctx.enter_context(tc.tile_pool(name="stage", bufs=3))
         cpool = ctx.enter_context(tc.tile_pool(name="codes", bufs=3))
         dcpool = ctx.enter_context(tc.tile_pool(name="dcodes", bufs=2))
         epool = ctx.enter_context(tc.tile_pool(name="epi", bufs=2))
-        opool = ctx.enter_context(tc.tile_pool(name="outs", bufs=4))
+        opool = ctx.enter_context(tc.tile_pool(name="outs", bufs=8))
         psum = ctx.enter_context(tc.psum_pool(name="psum", bufs=1))
         ctx.enter_context(tc.manual_schedule())
 
@@ -83,9 +83,9 @@ def tile_cudaternaryexpertmodule_kernel(
         nc.scalar.activation(out=warm_out[:], in_=warm[:], func=SILU)
 
         x_sb = []
-        for tt in range(4):
-            xt = const.tile([P, H], BF16, name="x%d" % tt)
-            nc.sync.dma_start(out=xt[:], in_=xf[P * tt : P * (tt + 1), :])
+        for c in range(2):
+            xt = const.tile([P, 2 * H], BF16, name="x%d" % c)
+            nc.sync.dma_start(out=xt[:], in_=x_rows[c])
             x_sb.append(xt)
 
         gw = {}
@@ -116,7 +116,6 @@ def tile_cudaternaryexpertmodule_kernel(
         xs = const.tile([P, 1024], U8, name="xs", align_bytes=64)
         hc = const.tile([P, G2 * 512], U32, name="hc", align_bytes=64)
         hs = const.tile([P, G2 * 512], U8, name="hs", align_bytes=64)
-        sc_w = const.tile([P, 24], F32, name="sc_w")
         sc_f = const.tile([P, 48], F32, name="sc_f")
 
         stg_of = {}
@@ -238,9 +237,12 @@ def tile_cudaternaryexpertmodule_kernel(
         dc_of = {}
 
         pdw = {}
+        pd_of = {}
 
         def permute_down(eng, dt, b, first, last):
-            pd = dppool.tile([P, INNER], BF16, name="pdw%d" % b, tag="pdw")
+            if b not in pd_of:
+                pd_of[b] = dppool.tile([P, INNER], BF16, name="pdw%d" % b, tag="pdw")
+            pd = pd_of[b]
             cols = slice(512 * first, 512 * last)
             eng.tensor_copy(
                 out=sorted_words(pd[:, cols].bitcast(dt), last - first),
@@ -297,14 +299,19 @@ def tile_cudaternaryexpertmodule_kernel(
                 out=o[:], in0=src, in1=ds_bc[:, 256 * q : 256 * (q + 1)], op=MULT
             )
             nc.sync.dma_start(
-                out=of[P * tt : P * (tt + 1), 256 * q : 256 * (q + 1)], in_=o[:]
+                out=out_rows[tt // 2, tt % 2][:, 256 * q : 256 * (q + 1)], in_=o[:]
             )
 
         xg = spool.tile([P, 4096], BF16, name="xg", tag="stg", align_bytes=64)
         xg4 = xg[:].bitcast(F32).rearrange("p (g w u) -> p g w u", g=2, w=TOK, u=2)
         for tt in range(4):
-            words = x_sb[tt][:].bitcast(F32)
-            srcs = [words[:, 256 * g + v : 256 * (g + 1) : 2] for g in range(2) for v in range(2)]
+            words = x_sb[tt // 2][:].bitcast(F32)
+            c0 = 512 * (tt % 2)
+            srcs = [
+                words[:, c0 + 256 * g + v : c0 + 256 * (g + 1) : 2]
+                for g in range(2)
+                for v in range(2)
+            ]
             bk = fill(tt, "tx%d" % tt, srcs)
             evac("v" if tt % 2 == 0 else "s", xg4[:, :, P * tt : P * (tt + 1), :], bk)
 
@@ -327,10 +334,9 @@ def tile_cudaternaryexpertmodule_kernel(
 
         bk = fill(7, "tsc", [sc_raw[:].bitcast(F32)[:, v:256:2] for v in range(2)])
         nc.vector.tensor_copy(
-            out=sc_w[:].rearrange("p (v r) -> p v r", v=2),
-            in_=bk[:, 0:256].rearrange("p (v r) -> p v r", v=2)[:, :, 0:12],
+            out=sc_f[:].rearrange("p (v c) -> p v c", v=2),
+            in_=bk[:, 0:256].bitcast(BF16).rearrange("p (v c) -> p v c", v=2)[:, :, 0:24],
         )
-        nc.vector.tensor_copy(out=sc_f[:], in_=sc_w[:].bitcast(BF16))
 
         early = ((0, 0), (0, 1), (0, 2), (0, 3), (0, 4), (0, 5), (1, 0), (1, 1))
         for a in range(UNITS):
@@ -362,26 +368,32 @@ def tile_cudaternaryexpertmodule_kernel(
             if a + 3 < UNITS:
                 permute_unit(a + 3)
             if a == 9:
-                permute_down(nc.gpsimd, U32, 2, 2, 6)
+                permute_down(nc.gpsimd, U32, 0, 0, 4)
+                permute_down(nc.vector, F32, 1, 0, 4)
             if a == 10:
-                permute_down(nc.gpsimd, U32, 3, 2, 6)
+                permute_down(nc.gpsimd, U32, 2, 2, 6)
+                permute_down(nc.vector, F32, 3, 2, 6)
             if a % 2 == 1:
                 regroup(a // 2)
 
-        tbks = [down_fill(1, g2, 2 + g2) for g2 in range(2, 6)]
-        for g2 in range(2, 6):
-            down_evac("s", 1, g2, tbks[g2 - 2])
+        obks = []
+        for tt in range(4):
+            ob = psum.tile([P, 512], F32, name="o0_%d" % tt, tag="bank%d" % tt)
+            obks.append(ob)
+        for g2 in (2, 3):
+            down_evac("s", 1, g2, down_fill(1, g2, 2 + g2))
+        for g2 in (0, 1):
+            for tt in range(4):
+                mx2_pass(0, tt, g2, obks[tt][:, 0:256])
+        for g2 in (4, 5):
+            down_evac("s", 1, g2, down_fill(1, g2, 2 + g2))
         down_quantise(0, 2)
         quantise_hidden(G2 - 1)
         down_quantise(1, 0)
         permute_down(nc.vector, F32, 4, 0, 6)
         permute_down(nc.vector, F32, 5, 0, 6)
 
-        obks = []
-        for tt in range(4):
-            ob = psum.tile([P, 512], F32, name="o0_%d" % tt, tag="bank%d" % tt)
-            obks.append(ob)
-        for g2 in range(G2):
+        for g2 in range(2, G2):
             for tt in range(4):
                 mx2_pass(0, tt, g2, obks[tt][:, 0:256])
         down_quantise(1, 1)
@@ -391,24 +403,20 @@ def tile_cudaternaryexpertmodule_kernel(
         permute_down(nc.vector, F32, 6, 0, 6)
         permute_down(nc.vector, F32, 7, 0, 6)
 
-        ring = (4, 5, 6, 7, 0, 1)
+        fill_banks = (4, 5, 6, 0, 1, 2)
+        out_banks = (7, 3)
         for q in (2, 3):
-            tbks = [down_fill(q, g2, ring[g2]) for g2 in range(G2)]
-            for g2 in range(G2):
-                down_evac("s", q, g2, tbks[g2])
-                if g2 == 3:
-                    down_quantise(q, 0)
-            down_quantise(q, 1)
-            down_quantise(q, 2)
-            obks = []
             for n in range(2):
-                ob = psum.tile([P, 512], F32, name="o%d_%d" % (q - 1, n), tag="bank%d" % (2 + n))
-                obks.append(ob)
+                for g2 in range(3 * n, 3 * n + 3):
+                    down_evac("s", q, g2, down_fill(q, g2, fill_banks[g2]))
+                    if g2 % 2 == 1:
+                        down_quantise(q, g2 // 2)
+                ob = psum.tile([P, 512], F32, name="o%d_%d" % (q - 1, n), tag="bank%d" % out_banks[n])
                 for half in range(2):
                     for g2 in range(G2):
                         mx2_pass(q - 1, 2 * n + half, g2, ob[:, 256 * half : 256 * (half + 1)])
-            for tt in range(4):
-                final(q - 1, tt, obks[tt // 2][:, 256 * (tt % 2) : 256 * (tt % 2 + 1)])
+                for half in range(2):
+                    final(q - 1, 2 * n + half, ob[:, 256 * half : 256 * (half + 1)])
 
         for tt in range(4):
             ob = psum.tile([P, 512], F32, name="o3_%d" % tt, tag="bank%d" % (4 + tt))

@@ -144,7 +144,7 @@ def tile_cudaternaryexpertmodule_kernel(
         def transpose_unit(a, banks):
             bks = []
             for j in range(4):
-                e, m = j // 2, j % 2
+                m, e = j // 2, j % 2
                 if a in perm_of:
                     words = perm_of[a][:].bitcast(F32)
                     c0 = 1024 * m + 512 * e
@@ -200,7 +200,7 @@ def tile_cudaternaryexpertmodule_kernel(
         def silu(a, e, bks):
             sl = epool.tile([P, 512], F32, name="sl%d_%d" % (a, e), tag="sl", bufs=3)
             c = 24 * (a % 2) + 2 * (a // 2) + e
-            nc.scalar.activation(out=sl[:], in_=bks[2 * e][:], func=SILU, scale=sc_f[:, c : c + 1])
+            nc.scalar.activation(out=sl[:], in_=bks[e][:], func=SILU, scale=sc_f[:, c : c + 1])
             sl_of[e] = sl
 
         def product(a, e, bks):
@@ -211,7 +211,7 @@ def tile_cudaternaryexpertmodule_kernel(
             c = 24 * (a % 2) + 12 + 2 * (a // 2) + e
             nc.vector.scalar_tensor_tensor(
                 out=hsb_of[a // 2][:, 512 * t : 512 * (t + 1)],
-                in0=bks[2 * e + 1][:],
+                in0=bks[2 + e][:],
                 scalar=sc_f[:, c : c + 1],
                 in1=sl_of[e][:],
                 op0=MULT,

from contextlib import ExitStack

import concourse.mybir as mybir
from concourse.masks import make_identity

F32 = mybir.dt.float32
BF16 = mybir.dt.bfloat16
U32 = mybir.dt.uint32
U8 = mybir.dt.uint8
FP8X4 = mybir.dt.float8_e4m3fn_x4
SILU = mybir.ActivationFunctionType.Silu
MULT = mybir.AluOpType.mult

P = 128
TOK = 512
H = 1024
INNER = 3072
UNITS = INNER // 256
G2 = INNER // 512
W_BUFS = 4
FLOPS = 2 * TOK * H * 2 * INNER + 2 * TOK * INNER * H


def tile_cudaternaryexpertmodule_kernel(
    tc, x, gate_w, up_w, down_w, gate_s, up_s, down_s, out
):
    nc = tc.nc
    x_rows = x.flatten_outer_dims().rearrange("(c p e) h -> c p (e h)", p=P, e=2)
    out_rows = out.flatten_outer_dims().rearrange("(c p e) h -> c e p h", p=P, e=2)
    gate_rows = gate_w.rearrange("(g p b e) h -> g b p (e h)", p=P, b=2, e=2)
    up_rows = up_w.rearrange("(g p b e) h -> g b p (e h)", p=P, b=2, e=2)
    down_rows = down_w.rearrange("(b p) k -> b p k", p=P)

    with ExitStack() as ctx:
        const = ctx.enter_context(tc.tile_pool(name="const", bufs=1))
        wpool = ctx.enter_context(tc.tile_pool(name="wpool", bufs=W_BUFS))
        dpool = ctx.enter_context(tc.tile_pool(name="dpool", bufs=8))
        dppool = ctx.enter_context(tc.tile_pool(name="dppool", bufs=6))
        spool = ctx.enter_context(tc.tile_pool(name="stage", bufs=3))
        cpool = ctx.enter_context(tc.tile_pool(name="codes", bufs=3))
        dcpool = ctx.enter_context(tc.tile_pool(name="dcodes", bufs=2))
        epool = ctx.enter_context(tc.tile_pool(name="epi", bufs=2))
        opool = ctx.enter_context(tc.tile_pool(name="outs", bufs=8))
        psum = ctx.enter_context(tc.psum_pool(name="psum", bufs=1))
        ctx.enter_context(tc.manual_schedule())

        def fill(bank_no, label, srcs):
            bk = psum.tile([P, 512], F32, name=label, tag="bank%d" % bank_no)
            for n, src in enumerate(srcs):
                nc.tensor.transpose(bk[:, P * n : P * (n + 1)], src, ident[:])
            return bk

        def evac(eng, dst4, bk):
            src4 = bk[:].rearrange("p (a u m) -> p a m u", a=2, u=2, m=P)
            if eng == "s":
                nc.scalar.copy(out=dst4, in_=src4)
            else:
                nc.vector.tensor_copy(out=dst4, in_=src4)

        def words512(stg, n):
            return (
                stg[:]
                .bitcast(F32)[:, 512 * n : 512 * (n + 1)]
                .rearrange("p (a m u) -> p a m u", a=2, m=P, u=2)
            )

        def quantise(stg, half, codes, scales, first_word):
            nc.vector.quantize_mx(
                out=codes[:, first_word : first_word + 512].bitcast(FP8X4),
                scales=scales[:, first_word : first_word + 512],
                in_=stg[:, 2048 * half : 2048 * (half + 1)],
            )

        warm = const.tile([P, 1], F32, name="warm")
        warm_out = const.tile([P, 1], F32, name="warm_out")
        nc.vector.memset(warm[:], 0.0)
        sc_raw = const.tile([P, 512], BF16, name="sc_raw")
        nc.vector.memset(sc_raw[:], 0.0)
        ident = const.tile([P, P], F32, name="ident")
        make_identity(nc, ident[:])
        nc.scalar.dma_start(out=sc_raw[0:6, :], in_=gate_s.rearrange("(a w) -> a w", a=G2))
        nc.scalar.dma_start(out=sc_raw[6:12, :], in_=up_s.rearrange("(a w) -> a w", a=G2))
        nc.scalar.activation(out=warm_out[:], in_=warm[:], func=SILU)

        x_sb = []
        for c in range(2):
            xt = const.tile([P, 2 * H], BF16, name="x%d" % c)
            nc.sync.dma_start(out=xt[:], in_=x_rows[c])
            x_sb.append(xt)

        gw = {}
        uw = {}

        def load_gu(a):
            g = wpool.tile([P, 2 * H], BF16, name="gw%d" % a, tag="gw")
            nc.sync.dma_start(out=g[:], in_=gate_rows[a // 2, a % 2])
            u = wpool.tile([P, 2 * H], BF16, name="uw%d" % a, tag="uw")
            nc.sync.dma_start(out=u[:], in_=up_rows[a // 2, a % 2])
            gw[a] = g
            uw[a] = u

        for a in range(W_BUFS):
            load_gu(a)

        dw = []
        ds_bc = const.tile([P, H], BF16, name="ds_bc")

        def load_down():
            for b in range(8):
                d = dpool.tile([P, INNER], BF16, name="dw%d" % b, tag="dw")
                nc.sync.dma_start(out=d[:], in_=down_rows[b])
                dw.append(d)
            nc.sync.dma_start(out=ds_bc[:], in_=down_s.partition_broadcast(P))

        xc = const.tile([P, 1024], U32, name="xc", align_bytes=64)
        xs = const.tile([P, 1024], U8, name="xs", align_bytes=64)
        hc = const.tile([P, G2 * 512], U32, name="hc", align_bytes=64)
        hs = const.tile([P, G2 * 512], U8, name="hs", align_bytes=64)
        sc_f = const.tile([P, 48], F32, name="sc_f")

        stg_of = {}
        wc_of = {}

        perm_of = {}

        def split_words(words, blocks):
            return words.rearrange("p (b w v) -> p b v w", b=blocks, w=P, v=2)

        def sorted_words(words, blocks):
            return words.rearrange("p (b v w) -> p b v w", b=blocks, v=2, w=P)

        def permute_unit(a):
            pp = spool.tile([P, 4096], BF16, name="pp%d" % a, tag="stg", align_bytes=64)
            nc.gpsimd.tensor_copy(
                out=sorted_words(pp[:, 2048:4096].bitcast(U32), 4),
                in_=split_words(uw[a][:].bitcast(U32), 4),
            )
            nc.vector.tensor_copy(
                out=sorted_words(pp[:, 0:2048].bitcast(F32), 4),
                in_=split_words(gw[a][:].bitcast(F32), 4),
            )
            perm_of[a] = pp

        def transpose_unit(a, banks):
            bks = []
            for j in range(4):
                m, e = j // 2, j % 2
                if a in perm_of:
                    words = perm_of[a][:].bitcast(F32)
                    c0 = 1024 * m + 512 * e
                    srcs = [words[:, c0 + P * n : c0 + P * (n + 1)] for n in range(4)]
                else:
                    words = (gw[a], uw[a])[m][:].bitcast(F32)
                    srcs = [
                        words[:, 512 * e + 256 * g + v : 512 * e + 256 * (g + 1) : 2]
                        for g in range(2)
                        for v in range(2)
                    ]
                bks.append(fill(banks[j], "t%d_%d" % (a, j), srcs))
            if a + W_BUFS < UNITS:
                load_gu(a + W_BUFS)
                if a + W_BUFS == UNITS - 1:
                    load_down()
            stg = spool.tile([P, 4096], BF16, name="stg%d" % a, tag="stg", align_bytes=64)
            stg_of[a] = stg
            return bks

        def new_codes(a):
            wc = cpool.tile([P, 1024], U32, name="wc%d" % a, tag="wc", align_bytes=64)
            ws = cpool.tile([P, 1024], U8, name="ws%d" % a, tag="ws", align_bytes=64)
            wc_of[a] = (wc, ws)

        def quantise_unit(a, half):
            wc, ws = wc_of[a]
            quantise(stg_of[a], half, wc, ws, 512 * half)

        def mx_unit(a):
            wc, ws = wc_of[a]
            bks = []
            for j in range(4):
                bk = psum.tile([P, 512], F32, name="m%d_%d" % (a, j), tag="bank%d" % (4 + j))
                for g in range(2):
                    c0 = 256 * j + P * g
                    nc.tensor.matmul_mx(
                        out=bk[:],
                        lhsT=wc[:, c0 : c0 + P].bitcast(FP8X4),
                        lhsT_scale=ws[:, c0 : c0 + P],
                        rhs=xc[:, 512 * g : 512 * (g + 1)].bitcast(FP8X4),
                        rhs_scale=xs[:, 512 * g : 512 * (g + 1)],
                        start=(g == 0),
                        stop=(g == 1),
                    )
                bks.append(bk)
            return bks

        sl_of = {}
        hsb_of = {}
        hg_of = {}

        def silu(a, e, bks):
            sl = epool.tile([P, 512], F32, name="sl%d_%d" % (a, e), tag="sl", bufs=3)
            c = 24 * (a % 2) + 2 * (a // 2) + e
            nc.scalar.activation(out=sl[:], in_=bks[e][:], func=SILU, scale=sc_f[:, c : c + 1])
            sl_of[e] = sl

        def product(a, e, bks):
            if a % 2 == 0 and e == 0:
                hsb = epool.tile([P, 2048], BF16, name="hsb%d" % (a // 2), tag="hsb")
                hsb_of[a // 2] = hsb
            t = 2 * (a % 2) + e
            c = 24 * (a % 2) + 12 + 2 * (a // 2) + e
            nc.vector.scalar_tensor_tensor(
                out=hsb_of[a // 2][:, 512 * t : 512 * (t + 1)],
                in0=bks[2 + e][:],
                scalar=sc_f[:, c : c + 1],
                in1=sl_of[e][:],
                op0=MULT,
                op1=MULT,
            )

        def regroup(g2):
            hg = epool.tile([P, 2048], BF16, name="hg%d" % g2, tag="hg", align_bytes=64)
            hg_of[g2] = hg
            dst = hg[:].rearrange("p (c i t) -> p c t i", c=P, i=4, t=4)
            src = hsb_of[g2][:].rearrange("p (t c i) -> p c t i", t=4, c=P, i=4)
            nc.vector.tensor_copy(out=dst[:, 0:64], in_=src[:, 0:64])
            nc.scalar.copy(out=dst[:, 64:128], in_=src[:, 64:128])

        def quantise_hidden(g2):
            nc.vector.quantize_mx(
                out=hc[:, 512 * g2 : 512 * (g2 + 1)].bitcast(FP8X4),
                scales=hs[:, 512 * g2 : 512 * (g2 + 1)],
                in_=hg_of[g2][:],
            )

        dstg_of = {}
        dc_of = {}

        pdw = {}
        pd_of = {}

        def permute_down(eng, dt, b, first, last):
            if b not in pd_of:
                pd_of[b] = dppool.tile([P, INNER], BF16, name="pdw%d" % b, tag="pdw")
            pd = pd_of[b]
            cols = slice(512 * first, 512 * last)
            eng.tensor_copy(
                out=sorted_words(pd[:, cols].bitcast(dt), last - first),
                in_=split_words(dw[b][:, cols].bitcast(dt), last - first),
            )
            for g2 in range(first, last):
                pdw[(b, g2)] = pd

        def down_fill(q, g2, bank_no):
            srcs = []
            for bb in range(2):
                b = 2 * q + bb
                for u in range(2):
                    if (b, g2) in pdw:
                        c0 = 256 * g2 + P * u
                        srcs.append(pdw[(b, g2)][:].bitcast(F32)[:, c0 : c0 + P])
                    else:
                        words = dw[b][:].bitcast(F32)
                        srcs.append(words[:, 256 * g2 + u : 256 * (g2 + 1) : 2])
            return fill(bank_no, "d%d_%d" % (q, g2), srcs)

        def down_evac(eng, q, g2, bk):
            if g2 % 4 == 0:
                stg = spool.tile(
                    [P, 4096], BF16, name="dstg%d_%d" % (q, g2 // 4), tag="stg", align_bytes=64
                )
                dstg_of[(q, g2 // 4)] = stg
            evac(eng, words512(dstg_of[(q, g2 // 4)], g2 % 4), bk)

        def down_quantise(q, pair):
            if pair == 0:
                dc = dcpool.tile([P, G2 * 256], U32, name="dc%d" % q, tag="dc", align_bytes=64)
                dsc = dcpool.tile([P, G2 * 256], U8, name="dsc%d" % q, tag="dsc", align_bytes=64)
                dc_of[q] = (dc, dsc)
            dc, dsc = dc_of[q]
            quantise(dstg_of[(q, pair // 2)], pair % 2, dc, dsc, 512 * pair)

        def mx2_pass(q, tt, g2, dst):
            dc, dsc = dc_of[q]
            c0 = 512 * g2 + P * tt
            nc.tensor.matmul_mx(
                out=dst,
                lhsT=hc[:, c0 : c0 + P].bitcast(FP8X4),
                lhsT_scale=hs[:, c0 : c0 + P],
                rhs=dc[:, 256 * g2 : 256 * (g2 + 1)].bitcast(FP8X4),
                rhs_scale=dsc[:, 256 * g2 : 256 * (g2 + 1)],
                start=(g2 == 0),
                stop=(g2 == G2 - 1),
            )

        def final(q, tt, src):
            o = opool.tile([P, 256], F32, name="o%d_%d" % (q, tt), tag="o")
            nc.vector.tensor_tensor(
                out=o[:], in0=src, in1=ds_bc[:, 256 * q : 256 * (q + 1)], op=MULT
            )
            nc.sync.dma_start(
                out=out_rows[tt // 2, tt % 2][:, 256 * q : 256 * (q + 1)], in_=o[:]
            )

        xg = spool.tile([P, 4096], BF16, name="xg", tag="stg", align_bytes=64)
        xg4 = xg[:].bitcast(F32).rearrange("p (g w u) -> p g w u", g=2, w=TOK, u=2)
        for tt in range(4):
            words = x_sb[tt // 2][:].bitcast(F32)
            c0 = 512 * (tt % 2)
            srcs = [
                words[:, c0 + 256 * g + v : c0 + 256 * (g + 1) : 2]
                for g in range(2)
                for v in range(2)
            ]
            bk = fill(tt, "tx%d" % tt, srcs)
            evac("v" if tt % 2 == 0 else "s", xg4[:, :, P * tt : P * (tt + 1), :], bk)

        quantise(xg, 0, xc, xs, 0)
        quantise(xg, 1, xc, xs, 512)

        bks = transpose_unit(0, (4, 5, 6, 7))
        new_codes(0)
        evac("s", words512(stg_of[0], 0), bks[0])
        evac("s", words512(stg_of[0], 1), bks[1])
        quantise_unit(0, 0)
        evac("s", words512(stg_of[0], 2), bks[2])
        evac("v", words512(stg_of[0], 3), bks[3])
        quantise_unit(0, 1)

        bks = transpose_unit(1, (0, 1, 2, 3))
        permute_unit(2)
        for j in range(4):
            evac("s", words512(stg_of[1], j), bks[j])

        bk = fill(7, "tsc", [sc_raw[:].bitcast(F32)[:, v:256:2] for v in range(2)])
        nc.vector.tensor_copy(
            out=sc_f[:].rearrange("p (v c) -> p v c", v=2),
            in_=bk[:, 0:256].bitcast(BF16).rearrange("p (v c) -> p v c", v=2)[:, :, 0:24],
        )

        early = ((0, 0), (0, 1), (0, 2), (0, 3), (0, 4), (0, 5), (1, 0), (1, 1))
        for a in range(UNITS):
            mbks = mx_unit(a)
            if a + 2 < UNITS:
                tbks = transpose_unit(a + 2, (0, 1, 2, 3))
            else:
                part = early[4 * (a - 10) : 4 * (a - 10) + 4]
                tbks = [down_fill(q, g2, n) for n, (q, g2) in enumerate(part)]
            silu(a, 0, mbks)
            silu(a, 1, mbks)
            for j in range(4):
                if a + 2 < UNITS:
                    evac("s", words512(stg_of[a + 2], j), tbks[j])
                else:
                    q, g2 = early[4 * (a - 10) + j]
                    down_evac("s", q, g2, tbks[j])
            if a + 1 < UNITS:
                new_codes(a + 1)
                quantise_unit(a + 1, 0)
                quantise_unit(a + 1, 1)
            else:
                down_quantise(0, 0)
                down_quantise(0, 1)
            if a % 2 == 0 and a >= 2:
                quantise_hidden(a // 2 - 1)
            product(a, 0, mbks)
            product(a, 1, mbks)
            if a + 3 < UNITS:
                permute_unit(a + 3)
            if a == 9:
                permute_down(nc.gpsimd, U32, 0, 0, 4)
                permute_down(nc.vector, F32, 1, 0, 4)
            if a == 10:
                permute_down(nc.gpsimd, U32, 2, 2, 6)
                permute_down(nc.vector, F32, 3, 2, 6)
            if a % 2 == 1:
                regroup(a // 2)

        obks = []
        for tt in range(4):
            ob = psum.tile([P, 512], F32, name="o0_%d" % tt, tag="bank%d" % tt)
            obks.append(ob)
        for g2 in (2, 3):
            down_evac("s", 1, g2, down_fill(1, g2, 2 + g2))
        for g2 in (0, 1):
            for tt in range(4):
                mx2_pass(0, tt, g2, obks[tt][:, 0:256])
        for g2 in (4, 5):
            down_evac("s", 1, g2, down_fill(1, g2, 2 + g2))
        down_quantise(0, 2)
        quantise_hidden(G2 - 1)
        down_quantise(1, 0)
        permute_down(nc.vector, F32, 4, 0, 6)
        permute_down(nc.vector, F32, 5, 0, 6)

        for g2 in range(2, G2):
            for tt in range(4):
                mx2_pass(0, tt, g2, obks[tt][:, 0:256])
        down_quantise(1, 1)
        down_quantise(1, 2)
        for tt in range(4):
            final(0, tt, obks[tt][:, 0:256])
        permute_down(nc.vector, F32, 6, 0, 6)
        permute_down(nc.vector, F32, 7, 0, 6)

        fill_banks = (4, 5, 6, 0, 1, 2)
        out_banks = (7, 3)
        for q in (2, 3):
            for n in range(2):
                for g2 in range(3 * n, 3 * n + 3):
                    down_evac("s", q, g2, down_fill(q, g2, fill_banks[g2]))
                    if g2 % 2 == 1:
                        down_quantise(q, g2 // 2)
                ob = psum.tile([P, 512], F32, name="o%d_%d" % (q - 1, n), tag="bank%d" % out_banks[n])
                for half in range(2):
                    for g2 in range(G2):
                        mx2_pass(q - 1, 2 * n + half, g2, ob[:, 256 * half : 256 * (half + 1)])
                for half in range(2):
                    final(q - 1, 2 * n + half, ob[:, 256 * half : 256 * (half + 1)])

        for tt in range(4):
            ob = psum.tile([P, 512], F32, name="o3_%d" % tt, tag="bank%d" % (4 + tt))
            for g2 in range(G2):
                mx2_pass(3, tt, g2, ob[:, 0:256])
            final(3, tt, ob[:, 0:256])
